import numpy as np
import ml_dtypes

BF16 = ml_dtypes.bfloat16


def bf(x):
    return np.asarray(x, np.float32).astype(BF16)


def f32(x):
    return np.asarray(x, np.float32)


def f64(x):
    return np.asarray(x).astype(np.float64)


def striped(idx):
    return np.tile(idx.reshape(-1, 16).T, (8, 1))


C, S, N, T = 128, 4096, 2048, 4


def setup_inputs():
    return {"src_enc": f32(np.random.standard_normal((C, S))), "t_emb": f32(np.random.standard_normal((C, T))), "w_in": bf(np.random.standard_normal((C, C)) / np.sqrt(C)), "b_in": f32(0.1 * np.random.standard_normal((C, 1))), "w_res": bf(np.random.standard_normal((C, C)) / np.sqrt(C)), "b_res": f32(0.1 * np.random.standard_normal((C, 1))), "offs": striped(np.random.permutation(np.tile(np.arange(S), 2))[:N])}


def reference(src_enc, t_emb, w_in, b_in, w_res, b_res, offs):
    idx = offs[:16].T.reshape(-1)
    emb = f64(src_enc)[:, idx][:, None, :] + f64(t_emb)[:, :, None]
    emb = emb.reshape(C, T * N)
    h = f64(w_in).T @ emb + f64(b_in)
    return f64(w_res).T @ h + f64(b_res)

@@ -1,0 +1,71 @@
+import concourse.mybir as mybir
+
+FP32 = mybir.dt.float32
+BF16 = mybir.dt.bfloat16
+U16 = mybir.dt.uint16
+ADD = mybir.AluOpType.add
+IDENTITY = mybir.ActivationFunctionType.Identity
+
+FEATURES = 128
+WORDS = 4096
+ENTRIES = 2048
+SYMBOLS = 4
+PIECE = 512
+PIECES = ENTRIES // PIECE
+OFFSET_COLUMNS = PIECE // 16
+
+FLOPS = 2 * 2 * FEATURES * FEATURES * SYMBOLS * ENTRIES
+
+
+def tile_synchpcfg_kernel(tc, src_enc, t_emb, w_in, b_in, w_res, b_res, offs, out):
+    nc = tc.nc
+    with (
+        tc.tile_pool(name="held", bufs=1) as held,
+        tc.tile_pool(name="ring", bufs=3) as ring,
+        tc.tile_pool(name="stores", bufs=8) as stores,
+        tc.psum_pool(name="psum", bufs=4) as psum,
+    ):
+        offsets = held.tile([FEATURES, ENTRIES // 16], U16, name="offsets")
+        symbols = held.tile([FEATURES, SYMBOLS], FP32, name="symbols")
+        table = held.tile([FEATURES, WORDS], FP32, name="table")
+        weights_in = held.tile([FEATURES, FEATURES], BF16, name="weights_in")
+        weights_res = held.tile([FEATURES, FEATURES], BF16, name="weights_res")
+        bias_in = held.tile([FEATURES, 1], FP32, name="bias_in")
+        bias_res = held.tile([FEATURES, 1], FP32, name="bias_res")
+
+        half = WORDS // 2
+        nc.sync.dma_start(offsets[:], offs)
+        nc.scalar.dma_start(symbols[:], t_emb)
+        nc.sync.dma_start(table[:, :half], src_enc[:, :half])
+        nc.scalar.dma_start(table[:, half:], src_enc[:, half:])
+        nc.sync.dma_start(weights_in[:], w_in)
+        nc.scalar.dma_start(bias_in[:], b_in)
+        nc.sync.dma_start(weights_res[:], w_res)
+        nc.scalar.dma_start(bias_res[:], b_res)
+
+        symbols_wide = held.tile([FEATURES, SYMBOLS, PIECE], FP32, name="symbols_wide")
+        for t in range(SYMBOLS):
+            nc.vector.tensor_copy(
+                symbols_wide[:, t, :], symbols[:, t : t + 1].to_broadcast([FEATURES, PIECE])
+            )
+
+        for t in range(SYMBOLS):
+            for p in range(PIECES):
+                picked = table[:].indirect(offsets[:, p * OFFSET_COLUMNS : (p + 1) * OFFSET_COLUMNS])
+                emb_fp32 = ring.tile([FEATURES, PIECE], FP32, name="emb_fp32")
+                nc.vector.tensor_tensor(emb_fp32[:], picked, symbols_wide[:, t, :], ADD)
+                emb = ring.tile([FEATURES, PIECE], BF16, name="emb")
+                nc.vector.tensor_copy(emb[:], emb_fp32[:])
+
+                h_bank = psum.tile([FEATURES, PIECE], FP32, name="h_bank")
+                nc.tensor.matmul(h_bank[:], weights_in[:], emb[:], start=True, stop=True)
+                h = ring.tile([FEATURES, PIECE], BF16, name="h")
+                nc.scalar.activation(h[:], h_bank[:], IDENTITY, bias=bias_in[:])
+
+                out_bank = psum.tile([FEATURES, PIECE], FP32, name="out_bank")
+                nc.tensor.matmul(out_bank[:], weights_res[:], h[:], start=True, stop=True)
+                result = stores.tile([FEATURES, PIECE], FP32, name="result")
+                nc.scalar.activation(result[:], out_bank[:], IDENTITY, bias=bias_res[:])
+
+                first = t * ENTRIES + p * PIECE
+                nc.sync.dma_start(out[:, first : first + PIECE], result[:])

@@ -49,23 +49,30 @@ def tile_synchpcfg_kernel(tc, src_enc, t_emb, w_in, b_in, w_res, b_res, offs, ou
                 symbols_wide[:, t, :], symbols[:, t : t + 1].to_broadcast([FEATURES, PIECE])
             )
 
-        for t in range(SYMBOLS):
-            for p in range(PIECES):
-                picked = table[:].indirect(offsets[:, p * OFFSET_COLUMNS : (p + 1) * OFFSET_COLUMNS])
-                emb_fp32 = ring.tile([FEATURES, PIECE], FP32, name="emb_fp32")
-                nc.vector.tensor_tensor(emb_fp32[:], picked, symbols_wide[:, t, :], ADD)
-                emb = ring.tile([FEATURES, PIECE], BF16, name="emb")
-                nc.vector.tensor_copy(emb[:], emb_fp32[:])
+        def first_layer(t, p):
+            picked = table[:].indirect(offsets[:, p * OFFSET_COLUMNS : (p + 1) * OFFSET_COLUMNS])
+            emb_fp32 = ring.tile([FEATURES, PIECE], FP32, name="emb_fp32")
+            nc.vector.tensor_tensor(emb_fp32[:], picked, symbols_wide[:, t, :], ADD)
+            emb = ring.tile([FEATURES, PIECE], BF16, name="emb")
+            nc.vector.tensor_copy(emb[:], emb_fp32[:])
+            h_bank = psum.tile([FEATURES, PIECE], FP32, name="h_bank")
+            nc.tensor.matmul(h_bank[:], weights_in[:], emb[:], start=True, stop=True)
+            h = ring.tile([FEATURES, PIECE], BF16, name="h")
+            nc.scalar.activation(h[:], h_bank[:], IDENTITY, bias=bias_in[:])
+            return h
 
-                h_bank = psum.tile([FEATURES, PIECE], FP32, name="h_bank")
-                nc.tensor.matmul(h_bank[:], weights_in[:], emb[:], start=True, stop=True)
-                h = ring.tile([FEATURES, PIECE], BF16, name="h")
-                nc.scalar.activation(h[:], h_bank[:], IDENTITY, bias=bias_in[:])
+        def second_layer(h, t, p):
+            out_bank = psum.tile([FEATURES, PIECE], FP32, name="out_bank")
+            nc.tensor.matmul(out_bank[:], weights_res[:], h[:], start=True, stop=True)
+            result = stores.tile([FEATURES, PIECE], FP32, name="result")
+            nc.scalar.activation(result[:], out_bank[:], IDENTITY, bias=bias_res[:])
+            first = t * ENTRIES + p * PIECE
+            nc.sync.dma_start(out[:, first : first + PIECE], result[:])
 
-                out_bank = psum.tile([FEATURES, PIECE], FP32, name="out_bank")
-                nc.tensor.matmul(out_bank[:], weights_res[:], h[:], start=True, stop=True)
-                result = stores.tile([FEATURES, PIECE], FP32, name="result")
-                nc.scalar.activation(result[:], out_bank[:], IDENTITY, bias=bias_res[:])
-
-                first = t * ENTRIES + p * PIECE
-                nc.sync.dma_start(out[:, first : first + PIECE], result[:])
+        units = [(t, p) for t in range(SYMBOLS) for p in range(PIECES)]
+        hidden = [first_layer(t, p) for t, p in units[:1]]
+        for (t, p), (t_next, p_next) in zip(units, units[1:]):
+            hidden.append(first_layer(t_next, p_next))
+            second_layer(hidden[-2], t, p)
+        t, p = units[-1]
+        second_layer(hidden[-1], t, p)

@@ -54,7 +54,7 @@ def tile_synchpcfg_kernel(tc, src_enc, t_emb, w_in, b_in, w_res, b_res, offs, ou
             emb_fp32 = ring.tile([FEATURES, PIECE], FP32, name="emb_fp32")
             nc.vector.tensor_tensor(emb_fp32[:], picked, symbols_wide[:, t, :], ADD)
             emb = ring.tile([FEATURES, PIECE], BF16, name="emb")
-            nc.vector.tensor_copy(emb[:], emb_fp32[:])
+            nc.gpsimd.tensor_copy(emb[:], emb_fp32[:])
             h_bank = psum.tile([FEATURES, PIECE], FP32, name="h_bank")
             nc.tensor.matmul(h_bank[:], weights_in[:], emb[:], start=True, stop=True)
             h = ring.tile([FEATURES, PIECE], BF16, name="h")

@@ -13,6 +13,7 @@ SYMBOLS = 4
 PIECE = 512
 PIECES = ENTRIES // PIECE
 OFFSET_COLUMNS = PIECE // 16
+LAG = 2
 
 FLOPS = 2 * 2 * FEATURES * FEATURES * SYMBOLS * ENTRIES
 
@@ -54,10 +55,10 @@ def tile_synchpcfg_kernel(tc, src_enc, t_emb, w_in, b_in, w_res, b_res, offs, ou
             emb_fp32 = ring.tile([FEATURES, PIECE], FP32, name="emb_fp32")
             nc.vector.tensor_tensor(emb_fp32[:], picked, symbols_wide[:, t, :], ADD)
             emb = ring.tile([FEATURES, PIECE], BF16, name="emb")
-            nc.gpsimd.tensor_copy(emb[:], emb_fp32[:])
+            nc.vector.tensor_copy(emb[:], emb_fp32[:])
             h_bank = psum.tile([FEATURES, PIECE], FP32, name="h_bank")
             nc.tensor.matmul(h_bank[:], weights_in[:], emb[:], start=True, stop=True)
-            h = ring.tile([FEATURES, PIECE], BF16, name="h")
+            h = ring.tile([FEATURES, PIECE], BF16, name="h", bufs=LAG + 2)
             nc.scalar.activation(h[:], h_bank[:], IDENTITY, bias=bias_in[:])
             return h
 
@@ -70,9 +71,11 @@ def tile_synchpcfg_kernel(tc, src_enc, t_emb, w_in, b_in, w_res, b_res, offs, ou
             nc.sync.dma_start(out[:, first : first + PIECE], result[:])
 
         units = [(t, p) for t in range(SYMBOLS) for p in range(PIECES)]
-        hidden = [first_layer(t, p) for t, p in units[:1]]
-        for (t, p), (t_next, p_next) in zip(units, units[1:]):
-            hidden.append(first_layer(t_next, p_next))
-            second_layer(hidden[-2], t, p)
-        t, p = units[-1]
-        second_layer(hidden[-1], t, p)
+        hidden = []
+        for i in range(len(units) + LAG):
+            if i < len(units):
+                t, p = units[i]
+                hidden.append(first_layer(t, p))
+            if i >= LAG:
+                t, p = units[i - LAG]
+                second_layer(hidden[i - LAG], t, p)

@@ -55,7 +55,10 @@ def tile_synchpcfg_kernel(tc, src_enc, t_emb, w_in, b_in, w_res, b_res, offs, ou
             emb_fp32 = ring.tile([FEATURES, PIECE], FP32, name="emb_fp32")
             nc.vector.tensor_tensor(emb_fp32[:], picked, symbols_wide[:, t, :], ADD)
             emb = ring.tile([FEATURES, PIECE], BF16, name="emb")
-            nc.vector.tensor_copy(emb[:], emb_fp32[:])
+            if p == 0:
+                nc.scalar.activation(emb[:], emb_fp32[:], IDENTITY)
+            else:
+                nc.vector.tensor_copy(emb[:], emb_fp32[:])
             h_bank = psum.tile([FEATURES, PIECE], FP32, name="h_bank")
             nc.tensor.matmul(h_bank[:], weights_in[:], emb[:], start=True, stop=True)
             h = ring.tile([FEATURES, PIECE], BF16, name="h", bufs=LAG + 2)

@@ -4,6 +4,7 @@ FP32 = mybir.dt.float32
 BF16 = mybir.dt.bfloat16
 U16 = mybir.dt.uint16
 ADD = mybir.AluOpType.add
+SUBTRACT = mybir.AluOpType.subtract
 IDENTITY = mybir.ActivationFunctionType.Identity
 
 FEATURES = 128
@@ -44,41 +45,46 @@ def tile_synchpcfg_kernel(tc, src_enc, t_emb, w_in, b_in, w_res, b_res, offs, ou
         nc.sync.dma_start(weights_res[:], w_res)
         nc.scalar.dma_start(bias_res[:], b_res)
 
-        symbols_wide = held.tile([FEATURES, SYMBOLS, PIECE], FP32, name="symbols_wide")
-        for t in range(SYMBOLS):
-            nc.vector.tensor_copy(
-                symbols_wide[:, t, :], symbols[:, t : t + 1].to_broadcast([FEATURES, PIECE])
-            )
+        symbol0_wide = held.tile([FEATURES, PIECE], FP32, name="symbol0_wide")
+        nc.vector.tensor_copy(symbol0_wide[:], symbols[:, 0:1].to_broadcast([FEATURES, PIECE]))
+        steps = held.tile([FEATURES, SYMBOLS], FP32, name="steps")
+        nc.vector.tensor_scalar(steps[:], symbols[:], symbols[:, 0:1], None, SUBTRACT)
 
-        def first_layer(t, p):
+        def look_up(p):
             picked = table[:].indirect(offsets[:, p * OFFSET_COLUMNS : (p + 1) * OFFSET_COLUMNS])
-            emb_fp32 = ring.tile([FEATURES, PIECE], FP32, name="emb_fp32")
-            nc.vector.tensor_tensor(emb_fp32[:], picked, symbols_wide[:, t, :], ADD)
+            emb0_fp32 = ring.tile([FEATURES, PIECE], FP32, name="emb0_fp32")
+            nc.vector.tensor_tensor(emb0_fp32[:], picked, symbol0_wide[:], ADD)
+            return emb0_fp32
+
+        def first_layer(emb0_fp32, t):
             emb = ring.tile([FEATURES, PIECE], BF16, name="emb")
-            if p == 0:
-                nc.scalar.activation(emb[:], emb_fp32[:], IDENTITY)
-            else:
-                nc.vector.tensor_copy(emb[:], emb_fp32[:])
+            nc.vector.tensor_scalar(emb[:], emb0_fp32[:], steps[:, t : t + 1], None, ADD)
             h_bank = psum.tile([FEATURES, PIECE], FP32, name="h_bank")
             nc.tensor.matmul(h_bank[:], weights_in[:], emb[:], start=True, stop=True)
             h = ring.tile([FEATURES, PIECE], BF16, name="h", bufs=LAG + 2)
             nc.scalar.activation(h[:], h_bank[:], IDENTITY, bias=bias_in[:])
             return h
 
-        def second_layer(h, t, p):
+        def second_layer(h, p, t):
             out_bank = psum.tile([FEATURES, PIECE], FP32, name="out_bank")
             nc.tensor.matmul(out_bank[:], weights_res[:], h[:], start=True, stop=True)
             result = stores.tile([FEATURES, PIECE], FP32, name="result")
-            nc.scalar.activation(result[:], out_bank[:], IDENTITY, bias=bias_res[:])
+            if t % 2 == 0:
+                nc.scalar.activation(result[:], out_bank[:], IDENTITY, bias=bias_res[:])
+            else:
+                nc.vector.tensor_scalar(result[:], out_bank[:], bias_res[:], None, ADD)
             first = t * ENTRIES + p * PIECE
             nc.sync.dma_start(out[:, first : first + PIECE], result[:])
 
-        units = [(t, p) for t in range(SYMBOLS) for p in range(PIECES)]
+        units = [(p, t) for p in range(PIECES) for t in range(SYMBOLS)]
         hidden = []
+        emb0_fp32 = None
         for i in range(len(units) + LAG):
             if i < len(units):
-                t, p = units[i]
-                hidden.append(first_layer(t, p))
+                p, t = units[i]
+                if t == 0:
+                    emb0_fp32 = look_up(p)
+                hidden.append(first_layer(emb0_fp32, t))
             if i >= LAG:
-                t, p = units[i - LAG]
-                second_layer(hidden[i - LAG], t, p)
+                p, t = units[i - LAG]
+                second_layer(hidden[i - LAG], p, t)

@@ -69,7 +69,7 @@ def tile_synchpcfg_kernel(tc, src_enc, t_emb, w_in, b_in, w_res, b_res, offs, ou
             out_bank = psum.tile([FEATURES, PIECE], FP32, name="out_bank")
             nc.tensor.matmul(out_bank[:], weights_res[:], h[:], start=True, stop=True)
             result = stores.tile([FEATURES, PIECE], FP32, name="result")
-            if t % 2 == 0:
+            if t == 0:
                 nc.scalar.activation(result[:], out_bank[:], IDENTITY, bias=bias_res[:])
             else:
                 nc.vector.tensor_scalar(result[:], out_bank[:], bias_res[:], None, ADD)

@@ -56,9 +56,12 @@ def tile_synchpcfg_kernel(tc, src_enc, t_emb, w_in, b_in, w_res, b_res, offs, ou
             nc.vector.tensor_tensor(emb0_fp32[:], picked, symbol0_wide[:], ADD)
             return emb0_fp32
 
-        def first_layer(emb0_fp32, t):
+        def first_layer(emb0_fp32, p, t):
             emb = ring.tile([FEATURES, PIECE], BF16, name="emb")
-            nc.vector.tensor_scalar(emb[:], emb0_fp32[:], steps[:, t : t + 1], None, ADD)
+            if p == 0 and t < 2:
+                nc.scalar.activation(emb[:], emb0_fp32[:], IDENTITY, bias=steps[:, t : t + 1])
+            else:
+                nc.vector.tensor_scalar(emb[:], emb0_fp32[:], steps[:, t : t + 1], None, ADD)
             h_bank = psum.tile([FEATURES, PIECE], FP32, name="h_bank")
             nc.tensor.matmul(h_bank[:], weights_in[:], emb[:], start=True, stop=True)
             h = ring.tile([FEATURES, PIECE], BF16, name="h", bufs=LAG + 2)
@@ -84,7 +87,7 @@ def tile_synchpcfg_kernel(tc, src_enc, t_emb, w_in, b_in, w_res, b_res, offs, ou
                 p, t = units[i]
                 if t == 0:
                     emb0_fp32 = look_up(p)
-                hidden.append(first_layer(emb0_fp32, t))
+                hidden.append(first_layer(emb0_fp32, p, t))
             if i >= LAG:
                 p, t = units[i - LAG]
                 second_layer(hidden[i - LAG], p, t)

@@ -72,7 +72,7 @@ def tile_synchpcfg_kernel(tc, src_enc, t_emb, w_in, b_in, w_res, b_res, offs, ou
             out_bank = psum.tile([FEATURES, PIECE], FP32, name="out_bank")
             nc.tensor.matmul(out_bank[:], weights_res[:], h[:], start=True, stop=True)
             result = stores.tile([FEATURES, PIECE], FP32, name="result")
-            if t == 0:
+            if t == (0 if p < PIECES - 1 else SYMBOLS - 1):
                 nc.scalar.activation(result[:], out_bank[:], IDENTITY, bias=bias_res[:])
             else:
                 nc.vector.tensor_scalar(result[:], out_bank[:], bias_res[:], None, ADD)

@@ -11,9 +11,8 @@ FEATURES = 128
 WORDS = 4096
 ENTRIES = 2048
 SYMBOLS = 4
-PIECE = 512
-PIECES = ENTRIES // PIECE
-OFFSET_COLUMNS = PIECE // 16
+UNIT = 512
+PIECES = ((0, 256), (256, 256), (512, 512), (1024, 512), (1536, 512))
 LAG = 2
 
 FLOPS = 2 * 2 * FEATURES * FEATURES * SYMBOLS * ENTRIES
@@ -45,49 +44,60 @@ def tile_synchpcfg_kernel(tc, src_enc, t_emb, w_in, b_in, w_res, b_res, offs, ou
         nc.sync.dma_start(weights_res[:], w_res)
         nc.scalar.dma_start(bias_res[:], b_res)
 
-        symbol0_wide = held.tile([FEATURES, PIECE], FP32, name="symbol0_wide")
-        nc.vector.tensor_copy(symbol0_wide[:], symbols[:, 0:1].to_broadcast([FEATURES, PIECE]))
+        symbol0_wide = held.tile([FEATURES, UNIT], FP32, name="symbol0_wide")
+        nc.vector.tensor_copy(symbol0_wide[:], symbols[:, 0:1].to_broadcast([FEATURES, UNIT]))
         steps = held.tile([FEATURES, SYMBOLS], FP32, name="steps")
         nc.vector.tensor_scalar(steps[:], symbols[:], symbols[:, 0:1], None, SUBTRACT)
 
         def look_up(p):
-            picked = table[:].indirect(offsets[:, p * OFFSET_COLUMNS : (p + 1) * OFFSET_COLUMNS])
-            emb0_fp32 = ring.tile([FEATURES, PIECE], FP32, name="emb0_fp32")
-            nc.vector.tensor_tensor(emb0_fp32[:], picked, symbol0_wide[:], ADD)
+            first, width = PIECES[p]
+            picked = table[:].indirect(offsets[:, first // 16 : (first + width) // 16])
+            emb0_fp32 = ring.tile([FEATURES, width], FP32, name="emb0_fp32")
+            nc.vector.tensor_tensor(emb0_fp32[:], picked, symbol0_wide[:, :width], ADD)
             return emb0_fp32
 
-        def first_layer(emb0_fp32, p, t):
-            emb = ring.tile([FEATURES, PIECE], BF16, name="emb")
-            if p == 0 and t < 2:
-                nc.scalar.activation(emb[:], emb0_fp32[:], IDENTITY, bias=steps[:, t : t + 1])
-            else:
-                nc.vector.tensor_scalar(emb[:], emb0_fp32[:], steps[:, t : t + 1], None, ADD)
-            h_bank = psum.tile([FEATURES, PIECE], FP32, name="h_bank")
+        def first_layer(emb0_fp32, p, unit_symbols):
+            first, width = PIECES[p]
+            emb = ring.tile([FEATURES, UNIT], BF16, name="emb")
+            for k, t in enumerate(unit_symbols):
+                emb_of_symbol = emb[:, k * width : (k + 1) * width]
+                if p == 0:
+                    nc.scalar.activation(emb_of_symbol, emb0_fp32[:], IDENTITY, bias=steps[:, t : t + 1])
+                else:
+                    nc.vector.tensor_scalar(emb_of_symbol, emb0_fp32[:], steps[:, t : t + 1], None, ADD)
+            h_bank = psum.tile([FEATURES, UNIT], FP32, name="h_bank")
             nc.tensor.matmul(h_bank[:], weights_in[:], emb[:], start=True, stop=True)
-            h = ring.tile([FEATURES, PIECE], BF16, name="h", bufs=LAG + 2)
+            h = ring.tile([FEATURES, UNIT], BF16, name="h", bufs=LAG + 2)
             nc.scalar.activation(h[:], h_bank[:], IDENTITY, bias=bias_in[:])
             return h
 
-        def second_layer(h, p, t):
-            out_bank = psum.tile([FEATURES, PIECE], FP32, name="out_bank")
+        def second_layer(h, p, unit_symbols):
+            first, width = PIECES[p]
+            out_bank = psum.tile([FEATURES, UNIT], FP32, name="out_bank")
             nc.tensor.matmul(out_bank[:], weights_res[:], h[:], start=True, stop=True)
-            result = stores.tile([FEATURES, PIECE], FP32, name="result")
-            if t == (0 if p < PIECES - 1 else SYMBOLS - 1):
+            result = stores.tile([FEATURES, UNIT], FP32, name="result")
+            if (unit_symbols[0] == 0) if p < len(PIECES) - 1 else (unit_symbols[-1] == SYMBOLS - 1):
                 nc.scalar.activation(result[:], out_bank[:], IDENTITY, bias=bias_res[:])
             else:
                 nc.vector.tensor_scalar(result[:], out_bank[:], bias_res[:], None, ADD)
-            first = t * ENTRIES + p * PIECE
-            nc.sync.dma_start(out[:, first : first + PIECE], result[:])
+            for k, t in enumerate(unit_symbols):
+                column = t * ENTRIES + first
+                nc.sync.dma_start(out[:, column : column + width], result[:, k * width : (k + 1) * width])
 
-        units = [(p, t) for p in range(PIECES) for t in range(SYMBOLS)]
+        units = []
+        for p, (first, width) in enumerate(PIECES):
+            symbols_in_unit = UNIT // width
+            for t in range(0, SYMBOLS, symbols_in_unit):
+                units.append((p, list(range(t, t + symbols_in_unit))))
+
         hidden = []
         emb0_fp32 = None
         for i in range(len(units) + LAG):
             if i < len(units):
-                p, t = units[i]
-                if t == 0:
+                p, unit_symbols = units[i]
+                if unit_symbols[0] == 0:
                     emb0_fp32 = look_up(p)
-                hidden.append(first_layer(emb0_fp32, p, t))
+                hidden.append(first_layer(emb0_fp32, p, unit_symbols))
             if i >= LAG:
-                p, t = units[i - LAG]
-                second_layer(hidden[i - LAG], p, t)
+                p, unit_symbols = units[i - LAG]
+                second_layer(hidden[i - LAG], p, unit_symbols)

@@ -76,7 +76,9 @@ def tile_synchpcfg_kernel(tc, src_enc, t_emb, w_in, b_in, w_res, b_res, offs, ou
             out_bank = psum.tile([FEATURES, UNIT], FP32, name="out_bank")
             nc.tensor.matmul(out_bank[:], weights_res[:], h[:], start=True, stop=True)
             result = stores.tile([FEATURES, UNIT], FP32, name="result")
-            if (unit_symbols[0] == 0) if p < len(PIECES) - 1 else (unit_symbols[-1] == SYMBOLS - 1):
+            first_of_four = first % UNIT == 0 and unit_symbols[0] == 0
+            last_of_four = unit_symbols[-1] == SYMBOLS - 1
+            if first_of_four if p < len(PIECES) - 1 else last_of_four:
                 nc.scalar.activation(result[:], out_bank[:], IDENTITY, bias=bias_res[:])
             else:
                 nc.vector.tensor_scalar(result[:], out_bank[:], bias_res[:], None, ADD)

@@ -4,6 +4,7 @@ FP32 = mybir.dt.float32
 BF16 = mybir.dt.bfloat16
 U16 = mybir.dt.uint16
 ADD = mybir.AluOpType.add
+MULT = mybir.AluOpType.mult
 SUBTRACT = mybir.AluOpType.subtract
 IDENTITY = mybir.ActivationFunctionType.Identity
 
@@ -15,6 +16,9 @@ UNIT = 512
 PIECES = ((0, 256), (256, 256), (512, 512), (1024, 512), (1536, 512))
 LAG = 2
 
+H_BANKS = 3
+OUT_BANKS = 5
+
 FLOPS = 2 * 2 * FEATURES * FEATURES * SYMBOLS * ENTRIES
 
 
@@ -24,7 +28,7 @@ def tile_synchpcfg_kernel(tc, src_enc, t_emb, w_in, b_in, w_res, b_res, offs, ou
         tc.tile_pool(name="held", bufs=1) as held,
         tc.tile_pool(name="ring", bufs=3) as ring,
         tc.tile_pool(name="stores", bufs=8) as stores,
-        tc.psum_pool(name="psum", bufs=4) as psum,
+        tc.psum_pool(name="psum", bufs=1) as psum,
     ):
         offsets = held.tile([FEATURES, ENTRIES // 16], U16, name="offsets")
         symbols = held.tile([FEATURES, SYMBOLS], FP32, name="symbols")
@@ -58,27 +62,27 @@ def tile_synchpcfg_kernel(tc, src_enc, t_emb, w_in, b_in, w_res, b_res, offs, ou
 
         def first_layer(emb0_fp32, p, unit_symbols):
             first, width = PIECES[p]
-            emb = ring.tile([FEATURES, UNIT], BF16, name="emb")
+            emb = ring.tile([FEATURES, UNIT], BF16, name="emb", bufs=8)
             for k, t in enumerate(unit_symbols):
                 emb_of_symbol = emb[:, k * width : (k + 1) * width]
                 if p == 0:
                     nc.scalar.activation(emb_of_symbol, emb0_fp32[:], IDENTITY, bias=steps[:, t : t + 1])
+                elif p >= len(PIECES) - 2:
+                    nc.gpsimd.tensor_scalar(emb_of_symbol, emb0_fp32[:], 1.0, steps[:, t : t + 1], MULT, ADD)
                 else:
                     nc.vector.tensor_scalar(emb_of_symbol, emb0_fp32[:], steps[:, t : t + 1], None, ADD)
-            h_bank = psum.tile([FEATURES, UNIT], FP32, name="h_bank")
+            h_bank = psum.tile([FEATURES, UNIT], FP32, name="h_bank", bufs=H_BANKS)
             nc.tensor.matmul(h_bank[:], weights_in[:], emb[:], start=True, stop=True)
             h = ring.tile([FEATURES, UNIT], BF16, name="h", bufs=LAG + 2)
             nc.scalar.activation(h[:], h_bank[:], IDENTITY, bias=bias_in[:])
             return h
 
-        def second_layer(h, p, unit_symbols):
+        def second_layer(h, i, p, unit_symbols):
             first, width = PIECES[p]
-            out_bank = psum.tile([FEATURES, UNIT], FP32, name="out_bank")
+            out_bank = psum.tile([FEATURES, UNIT], FP32, name="out_bank", bufs=OUT_BANKS)
             nc.tensor.matmul(out_bank[:], weights_res[:], h[:], start=True, stop=True)
             result = stores.tile([FEATURES, UNIT], FP32, name="result")
-            first_of_four = first % UNIT == 0 and unit_symbols[0] == 0
-            last_of_four = unit_symbols[-1] == SYMBOLS - 1
-            if first_of_four if p < len(PIECES) - 1 else last_of_four:
+            if i % 8 == 0:
                 nc.scalar.activation(result[:], out_bank[:], IDENTITY, bias=bias_res[:])
             else:
                 nc.vector.tensor_scalar(result[:], out_bank[:], bias_res[:], None, ADD)
@@ -102,4 +106,4 @@ def tile_synchpcfg_kernel(tc, src_enc, t_emb, w_in, b_in, w_res, b_res, offs, ou
                 hidden.append(first_layer(emb0_fp32, p, unit_symbols))
             if i >= LAG:
                 p, unit_symbols = units[i - LAG]
-                second_layer(hidden[i - LAG], p, unit_symbols)
+                second_layer(hidden[i - LAG], i - LAG, p, unit_symbols)

@@ -13,7 +13,7 @@ WORDS = 4096
 ENTRIES = 2048
 SYMBOLS = 4
 UNIT = 512
-PIECES = ((0, 256), (256, 256), (512, 512), (1024, 512), (1536, 512))
+PIECES = ((0, 256), (256, 256), (512, 512), (1024, 1024))
 LAG = 2
 
 H_BANKS = 3
@@ -48,8 +48,8 @@ def tile_synchpcfg_kernel(tc, src_enc, t_emb, w_in, b_in, w_res, b_res, offs, ou
         nc.sync.dma_start(weights_res[:], w_res)
         nc.scalar.dma_start(bias_res[:], b_res)
 
-        symbol0_wide = held.tile([FEATURES, UNIT], FP32, name="symbol0_wide")
-        nc.vector.tensor_copy(symbol0_wide[:], symbols[:, 0:1].to_broadcast([FEATURES, UNIT]))
+        symbol0_wide = held.tile([FEATURES, 2 * UNIT], FP32, name="symbol0_wide")
+        nc.vector.tensor_copy(symbol0_wide[:], symbols[:, 0:1].to_broadcast([FEATURES, 2 * UNIT]))
         steps = held.tile([FEATURES, SYMBOLS], FP32, name="steps")
         nc.vector.tensor_scalar(steps[:], symbols[:], symbols[:, 0:1], None, SUBTRACT)
 
@@ -60,50 +60,56 @@ def tile_synchpcfg_kernel(tc, src_enc, t_emb, w_in, b_in, w_res, b_res, offs, ou
             nc.vector.tensor_tensor(emb0_fp32[:], picked, symbol0_wide[:, :width], ADD)
             return emb0_fp32
 
-        def first_layer(emb0_fp32, p, unit_symbols):
+        def embed(emb0_fp32, p, group):
             first, width = PIECES[p]
-            emb = ring.tile([FEATURES, UNIT], BF16, name="emb", bufs=8)
-            for k, t in enumerate(unit_symbols):
+            emb = ring.tile([FEATURES, width * len(group)], BF16, name="emb", bufs=8)
+            for k, t in enumerate(group):
                 emb_of_symbol = emb[:, k * width : (k + 1) * width]
                 if p == 0:
                     nc.scalar.activation(emb_of_symbol, emb0_fp32[:], IDENTITY, bias=steps[:, t : t + 1])
-                elif p >= len(PIECES) - 2:
+                elif p == len(PIECES) - 1:
                     nc.gpsimd.tensor_scalar(emb_of_symbol, emb0_fp32[:], 1.0, steps[:, t : t + 1], MULT, ADD)
                 else:
                     nc.vector.tensor_scalar(emb_of_symbol, emb0_fp32[:], steps[:, t : t + 1], None, ADD)
+            return emb
+
+        def first_layer(emb_of_unit):
             h_bank = psum.tile([FEATURES, UNIT], FP32, name="h_bank", bufs=H_BANKS)
-            nc.tensor.matmul(h_bank[:], weights_in[:], emb[:], start=True, stop=True)
+            nc.tensor.matmul(h_bank[:], weights_in[:], emb_of_unit, start=True, stop=True)
             h = ring.tile([FEATURES, UNIT], BF16, name="h", bufs=LAG + 2)
             nc.scalar.activation(h[:], h_bank[:], IDENTITY, bias=bias_in[:])
             return h
 
-        def second_layer(h, i, p, unit_symbols):
+        def second_layer(h, i, unit):
+            p, group, part = unit
             first, width = PIECES[p]
             out_bank = psum.tile([FEATURES, UNIT], FP32, name="out_bank", bufs=OUT_BANKS)
             nc.tensor.matmul(out_bank[:], weights_res[:], h[:], start=True, stop=True)
             result = stores.tile([FEATURES, UNIT], FP32, name="result")
-            if i % 8 == 0:
+            if i % 4 == 0 and p < len(PIECES) - 1:
                 nc.scalar.activation(result[:], out_bank[:], IDENTITY, bias=bias_res[:])
             else:
                 nc.vector.tensor_scalar(result[:], out_bank[:], bias_res[:], None, ADD)
-            for k, t in enumerate(unit_symbols):
-                column = t * ENTRIES + first
-                nc.sync.dma_start(out[:, column : column + width], result[:, k * width : (k + 1) * width])
+            run = min(width, UNIT)
+            for k, t in enumerate(group):
+                column = t * ENTRIES + first + part * UNIT
+                nc.sync.dma_start(out[:, column : column + run], result[:, k * run : (k + 1) * run])
 
         units = []
         for p, (first, width) in enumerate(PIECES):
-            symbols_in_unit = UNIT // width
-            for t in range(0, SYMBOLS, symbols_in_unit):
-                units.append((p, list(range(t, t + symbols_in_unit))))
+            group_size = max(1, UNIT // width)
+            for t in range(0, SYMBOLS, group_size):
+                for part in range(max(1, width // UNIT)):
+                    units.append((p, tuple(range(t, t + group_size)), part))
 
         hidden = []
-        emb0_fp32 = None
         for i in range(len(units) + LAG):
             if i < len(units):
-                p, unit_symbols = units[i]
-                if unit_symbols[0] == 0:
+                p, group, part = units[i]
+                if group[0] == 0 and part == 0:
                     emb0_fp32 = look_up(p)
-                hidden.append(first_layer(emb0_fp32, p, unit_symbols))
+                if part == 0:
+                    emb = embed(emb0_fp32, p, group)
+                hidden.append(first_layer(emb[:, part * UNIT : (part + 1) * UNIT]))
             if i >= LAG:
-                p, unit_symbols = units[i - LAG]
-                second_layer(hidden[i - LAG], i - LAG, p, unit_symbols)
+                second_layer(hidden[i - LAG], i - LAG, units[i - LAG])

@@ -13,7 +13,7 @@ WORDS = 4096
 ENTRIES = 2048
 SYMBOLS = 4
 UNIT = 512
-PIECES = ((0, 256), (256, 256), (512, 512), (1024, 1024))
+PIECES = ((0, 512), (512, 512), (1024, 1024))
 LAG = 2
 
 H_BANKS = 3
@@ -56,16 +56,16 @@ def tile_synchpcfg_kernel(tc, src_enc, t_emb, w_in, b_in, w_res, b_res, offs, ou
         def look_up(p):
             first, width = PIECES[p]
             picked = table[:].indirect(offsets[:, first // 16 : (first + width) // 16])
-            emb0_fp32 = ring.tile([FEATURES, width], FP32, name="emb0_fp32")
+            emb0_fp32 = ring.tile([FEATURES, width], FP32, name="emb0_fp32", bufs=2)
             nc.vector.tensor_tensor(emb0_fp32[:], picked, symbol0_wide[:, :width], ADD)
             return emb0_fp32
 
-        def embed(emb0_fp32, p, group):
+        def embed(emb0_fp32, i, p, group):
             first, width = PIECES[p]
             emb = ring.tile([FEATURES, width * len(group)], BF16, name="emb", bufs=8)
             for k, t in enumerate(group):
                 emb_of_symbol = emb[:, k * width : (k + 1) * width]
-                if p == 0:
+                if i < LAG:
                     nc.scalar.activation(emb_of_symbol, emb0_fp32[:], IDENTITY, bias=steps[:, t : t + 1])
                 elif p == len(PIECES) - 1:
                     nc.gpsimd.tensor_scalar(emb_of_symbol, emb0_fp32[:], 1.0, steps[:, t : t + 1], MULT, ADD)
@@ -109,7 +109,7 @@ def tile_synchpcfg_kernel(tc, src_enc, t_emb, w_in, b_in, w_res, b_res, offs, ou
                 if group[0] == 0 and part == 0:
                     emb0_fp32 = look_up(p)
                 if part == 0:
-                    emb = embed(emb0_fp32, p, group)
+                    emb = embed(emb0_fp32, i, p, group)
                 hidden.append(first_layer(emb[:, part * UNIT : (part + 1) * UNIT]))
             if i >= LAG:
                 second_layer(hidden[i - LAG], i - LAG, units[i - LAG])

@@ -38,11 +38,9 @@ def tile_synchpcfg_kernel(tc, src_enc, t_emb, w_in, b_in, w_res, b_res, offs, ou
         bias_in = held.tile([FEATURES, 1], FP32, name="bias_in")
         bias_res = held.tile([FEATURES, 1], FP32, name="bias_res")
 
-        half = WORDS // 2
         nc.sync.dma_start(offsets[:], offs)
         nc.scalar.dma_start(symbols[:], t_emb)
-        nc.sync.dma_start(table[:, :half], src_enc[:, :half])
-        nc.scalar.dma_start(table[:, half:], src_enc[:, half:])
+        nc.sync.dma_start(table[:], src_enc)
         nc.sync.dma_start(weights_in[:], w_in)
         nc.scalar.dma_start(bias_in[:], b_in)
         nc.sync.dma_start(weights_res[:], w_res)

import concourse.mybir as mybir

FP32 = mybir.dt.float32
BF16 = mybir.dt.bfloat16
U16 = mybir.dt.uint16
ADD = mybir.AluOpType.add
MULT = mybir.AluOpType.mult
SUBTRACT = mybir.AluOpType.subtract
IDENTITY = mybir.ActivationFunctionType.Identity

FEATURES = 128
WORDS = 4096
ENTRIES = 2048
SYMBOLS = 4
UNIT = 512
PIECES = ((0, 512), (512, 512), (1024, 1024))
LAG = 2

H_BANKS = 3
OUT_BANKS = 5

FLOPS = 2 * 2 * FEATURES * FEATURES * SYMBOLS * ENTRIES


def tile_synchpcfg_kernel(tc, src_enc, t_emb, w_in, b_in, w_res, b_res, offs, out):
    nc = tc.nc
    with (
        tc.tile_pool(name="held", bufs=1) as held,
        tc.tile_pool(name="ring", bufs=3) as ring,
        tc.tile_pool(name="stores", bufs=8) as stores,
        tc.psum_pool(name="psum", bufs=1) as psum,
    ):
        offsets = held.tile([FEATURES, ENTRIES // 16], U16, name="offsets")
        symbols = held.tile([FEATURES, SYMBOLS], FP32, name="symbols")
        table = held.tile([FEATURES, WORDS], FP32, name="table")
        weights_in = held.tile([FEATURES, FEATURES], BF16, name="weights_in")
        weights_res = held.tile([FEATURES, FEATURES], BF16, name="weights_res")
        bias_in = held.tile([FEATURES, 1], FP32, name="bias_in")
        bias_res = held.tile([FEATURES, 1], FP32, name="bias_res")

        nc.sync.dma_start(offsets[:], offs)
        nc.scalar.dma_start(symbols[:], t_emb)
        nc.sync.dma_start(table[:], src_enc)
        nc.sync.dma_start(weights_in[:], w_in)
        nc.scalar.dma_start(bias_in[:], b_in)
        nc.sync.dma_start(weights_res[:], w_res)
        nc.scalar.dma_start(bias_res[:], b_res)

        symbol0_wide = held.tile([FEATURES, 2 * UNIT], FP32, name="symbol0_wide")
        nc.vector.tensor_copy(symbol0_wide[:], symbols[:, 0:1].to_broadcast([FEATURES, 2 * UNIT]))
        steps = held.tile([FEATURES, SYMBOLS], FP32, name="steps")
        nc.vector.tensor_scalar(steps[:], symbols[:], symbols[:, 0:1], None, SUBTRACT)

        def look_up(p):
            first, width = PIECES[p]
            picked = table[:].indirect(offsets[:, first // 16 : (first + width) // 16])
            emb0_fp32 = ring.tile([FEATURES, width], FP32, name="emb0_fp32", bufs=2)
            nc.vector.tensor_tensor(emb0_fp32[:], picked, symbol0_wide[:, :width], ADD)
            return emb0_fp32

        def embed(emb0_fp32, i, p, group):
            first, width = PIECES[p]
            emb = ring.tile([FEATURES, width * len(group)], BF16, name="emb", bufs=8)
            for k, t in enumerate(group):
                emb_of_symbol = emb[:, k * width : (k + 1) * width]
                if i < LAG:
                    nc.scalar.activation(emb_of_symbol, emb0_fp32[:], IDENTITY, bias=steps[:, t : t + 1])
                elif p == len(PIECES) - 1:
                    nc.gpsimd.tensor_scalar(emb_of_symbol, emb0_fp32[:], 1.0, steps[:, t : t + 1], MULT, ADD)
                else:
                    nc.vector.tensor_scalar(emb_of_symbol, emb0_fp32[:], steps[:, t : t + 1], None, ADD)
            return emb

        def first_layer(emb_of_unit):
            h_bank = psum.tile([FEATURES, UNIT], FP32, name="h_bank", bufs=H_BANKS)
            nc.tensor.matmul(h_bank[:], weights_in[:], emb_of_unit, start=True, stop=True)
            h = ring.tile([FEATURES, UNIT], BF16, name="h", bufs=LAG + 2)
            nc.scalar.activation(h[:], h_bank[:], IDENTITY, bias=bias_in[:])
            return h

        def second_layer(h, i, unit):
            p, group, part = unit
            first, width = PIECES[p]
            out_bank = psum.tile([FEATURES, UNIT], FP32, name="out_bank", bufs=OUT_BANKS)
            nc.tensor.matmul(out_bank[:], weights_res[:], h[:], start=True, stop=True)
            result = stores.tile([FEATURES, UNIT], FP32, name="result")
            if i % 4 == 0 and p < len(PIECES) - 1:
                nc.scalar.activation(result[:], out_bank[:], IDENTITY, bias=bias_res[:])
            else:
                nc.vector.tensor_scalar(result[:], out_bank[:], bias_res[:], None, ADD)
            run = min(width, UNIT)
            for k, t in enumerate(group):
                column = t * ENTRIES + first + part * UNIT
                nc.sync.dma_start(out[:, column : column + run], result[:, k * run : (k + 1) * run])

        units = []
        for p, (first, width) in enumerate(PIECES):
            group_size = max(1, UNIT // width)
            for t in range(0, SYMBOLS, group_size):
                for part in range(max(1, width // UNIT)):
                    units.append((p, tuple(range(t, t + group_size)), part))

        hidden = []
        for i in range(len(units) + LAG):
            if i < len(units):
                p, group, part = units[i]
                if group[0] == 0 and part == 0:
                    emb0_fp32 = look_up(p)
                if part == 0:
                    emb = embed(emb0_fp32, i, p, group)
                hidden.append(first_layer(emb[:, part * UNIT : (part + 1) * UNIT]))
            if i >= LAG:
                second_layer(hidden[i - LAG], i - LAG, units[i - LAG])
